import numpy as np
import ml_dtypes


def mxq(x, axis, fmt="e4m3"):
    dtype, down = {"e4m3": (ml_dtypes.float8_e4m3fn, 7), "e5m2": (ml_dtypes.float8_e5m2, 14)}[fmt]
    v = np.moveaxis(np.asarray(x, np.float32).astype(ml_dtypes.bfloat16).astype(np.float64), axis, -1)
    blocks = v.reshape(v.shape[:-1] + (-1, 32))
    amax = np.abs(blocks).max(-1, keepdims=True)
    byte = np.maximum(np.where(amax > 0, np.frexp(amax)[1] - 1 + 127, 0) - down, 1)
    scale = np.exp2(byte - 127.0)
    codes = (blocks / scale).astype(np.float32).astype(dtype).astype(np.float64)
    return np.moveaxis((codes * scale).reshape(v.shape), -1, axis)


WIDE = False


def mx_kscale(k):
    if not WIDE:
        return np.ones(k)
    levels = np.array([10, -10, 5, -5, 0])
    if k % 512:
        return np.exp2(np.random.permutation(np.resize(levels, k // 32))).repeat(32)
    a = np.empty((k // 512, 16))
    for p in range(k // 512):
        a[p, :8] = np.random.permutation(np.resize(levels, 8))
        for g in range(8):
            far = levels[np.abs(levels - a[p, g]) >= 10]
            a[p, g + 8] = far[np.random.randint(len(far))]
    return np.exp2(a.ravel()).repeat(32)


BF16 = ml_dtypes.bfloat16


def bf(x):
    return np.asarray(x, np.float32).astype(BF16)


def f64(x):
    return np.asarray(x).astype(np.float64)


N, V, EN1, EN2, D, K, EMB = 1024, 4096, 1024, 512, 128, 512, 1024
BN_EPS = 1e-5


def batchnorm(x):
    m = x.mean(axis=0)
    v = x.var(axis=0)
    return (x - m) * (1.0 / np.sqrt(v + BN_EPS))


def setup_inputs():
    s, t = mx_kscale(EN1), mx_kscale(EN2)
    return {
        "en1": bf(np.maximum(np.random.standard_normal((N, EN1)) * 1.15, 0.0) * s),
        "W2": bf(np.random.standard_normal((EN1, EN2)) / np.sqrt(EN1) / s[:, None] * t),
        "b2": bf(np.random.standard_normal(EN2) * 0.2 * t),
        "Wmean": bf(np.random.standard_normal((EN2, D)) / np.sqrt(EN2) / t[:, None]),
        "Wlogvar": bf(np.random.standard_normal((EN2, D)) / np.sqrt(EN2) / t[:, None]),
        "eps": bf(np.random.standard_normal((N, D))),
    }


def reference(en1, W2, b2, Wmean, Wlogvar, eps):
    en2 = np.maximum((mxq(f64(en1), 1, "e4m3") @ mxq(f64(W2), 0, "e4m3")) + f64(b2), 0.0)
    en2q = mxq(en2, 1, "e4m3")
    posterior_mean = batchnorm(en2q @ mxq(f64(Wmean), 0, "e4m3"))
    posterior_logvar = batchnorm(en2q @ mxq(f64(Wlogvar), 0, "e4m3"))
    posterior_var = np.exp(posterior_logvar)
    z = posterior_mean + np.sqrt(posterior_var) * f64(eps)
    zx = batchnorm(z)
    return z, zx

@@ -1,0 +1,299 @@
+from contextlib import ExitStack
+
+import concourse.mybir as mybir
+from concourse.masks import make_identity
+
+F32 = mybir.dt.float32
+BF16 = mybir.dt.bfloat16
+U32 = mybir.dt.uint32
+U8 = mybir.dt.uint8
+FP8X4 = mybir.dt.float8_e4m3fn_x4
+ALU = mybir.AluOpType
+ACT = mybir.ActivationFunctionType
+
+P = 128
+PACK = 4
+K_PASS = P * PACK
+
+ROWS, EN1, EN2, D = 1024, 1024, 512, 128
+BN_EPS = 1e-5
+
+CHUNKS = ROWS // P
+BANK = 512
+BANKS = ROWS // BANK
+CHUNKS_PER_BANK = BANK // P
+STAGE = 256
+STAGES = ROWS // STAGE
+CHUNKS_PER_STAGE = STAGE // P
+STAGES_PER_BANK = BANK // STAGE
+PASSES1 = EN1 // K_PASS
+E_TILES = EN2 // P
+HALVES = 2
+RUN = 4
+
+MEAN, LOGVAR, SAMPLE = 0, 1, 2
+BN_STATS_DIM = 6
+
+FLOPS = 2 * ROWS * EN1 * EN2 + 2 * 2 * ROWS * EN2 * D
+
+
+def regroup(copy, grouped, planes):
+    copy(
+        out=grouped.rearrange("p (c i) t -> p c t i", i=RUN),
+        in_=planes.rearrange("p t (c i) -> p c t i", i=RUN),
+    )
+
+
+def tile_modelvd_pa_kernel(tc, en1, W2, b2, Wmean, Wlogvar, eps, out_0, out_1):
+    nc = tc.nc
+    with ExitStack() as ctx:
+        ctx.enter_context(tc.manual_schedule())
+        keep = ctx.enter_context(tc.tile_pool(name="keep", bufs=1))
+        stage_pool = ctx.enter_context(tc.tile_pool(name="stage_pool", bufs=2))
+        rows_pool = ctx.enter_context(tc.tile_pool(name="rows_pool", bufs=2 * BANKS))
+        psum_flip = ctx.enter_context(tc.psum_pool(name="psum_flip", bufs=4))
+        psum_acc = ctx.enter_context(tc.psum_pool(name="psum_acc", bufs=4))
+
+        ident_f32 = keep.tile([P, P], F32)
+        make_identity(nc, ident_f32[:])
+        ident_bf16 = keep.tile([P, P], BF16)
+        make_identity(nc, ident_bf16[:])
+        minus_half = keep.tile([P, 1], F32)
+        nc.vector.memset(minus_half[:], -0.5)
+        table_warmer = keep.tile([P, 1], F32)
+        nc.scalar.activation(out=table_warmer[:], in_=minus_half[:], func=ACT.Exp)
+
+        w2_raw = keep.tile([P, PASSES1, PACK, EN2], BF16)
+        for g in range(PASSES1):
+            nc.sync.dma_start(
+                out=w2_raw[:, g],
+                in_=W2[g * K_PASS : (g + 1) * K_PASS, :].rearrange("(q j) c -> q j c", j=PACK),
+            )
+        b2_raw = keep.tile([P, E_TILES], BF16)
+        nc.sync.dma_start(out=b2_raw[:], in_=b2.rearrange("(p t) -> p t", t=E_TILES))
+        en1_sb = keep.tile([P, CHUNKS, EN1], BF16)
+        en1_rows = en1.rearrange("(p c) k -> p c k", c=CHUNKS)
+        head_raw = keep.tile([P, 2, PACK, D], BF16)
+        eps_sb = keep.tile([P, CHUNKS, D], BF16)
+
+        def load_en1(s):
+            chunks = slice(s * CHUNKS_PER_STAGE, (s + 1) * CHUNKS_PER_STAGE)
+            nc.sync.dma_start(out=en1_sb[:, chunks, :], in_=en1_rows[:, chunks, :])
+
+        load_en1(0)
+        load_en1(1)
+        nc.sync.dma_start(out=head_raw[:, MEAN], in_=Wmean.rearrange("(p t) d -> p t d", t=PACK))
+        nc.sync.dma_start(out=head_raw[:, LOGVAR], in_=Wlogvar.rearrange("(p t) d -> p t d", t=PACK))
+        load_en1(2)
+        load_en1(3)
+        nc.sync.dma_start(out=eps_sb[:], in_=eps.rearrange("(p c) d -> p c d", c=CHUNKS))
+
+        w2_grouped = keep.tile([P, PASSES1, EN2, PACK], BF16, align_bytes=64)
+        w2_codes = keep.tile([P, PASSES1, EN2], U32, align_bytes=64)
+        w2_scales = keep.tile([P, PASSES1, EN2], U8, align_bytes=64)
+        for g in range(PASSES1):
+            grouped = w2_grouped[:, g].rearrange("q (t m) j -> q m j t", t=E_TILES)
+            raw = w2_raw[:, g].rearrange("q j (m t) -> q m j t", t=E_TILES)
+            half = P // 2
+            nc.vector.tensor_copy(out=grouped[:, 0:half], in_=raw[:, 0:half])
+            nc.scalar.copy(out=grouped[:, half:P], in_=raw[:, half:P])
+        for g in range(PASSES1):
+            nc.vector.quantize_mx(
+                out=w2_codes[:, g, :].bitcast(FP8X4),
+                scales=w2_scales[:, g, :],
+                in_=w2_grouped[:, g].rearrange("q c t -> q (c t)"),
+            )
+
+        head_codes = keep.tile([P, 2, D], U32, align_bytes=64)
+        head_scales = keep.tile([P, 2, D], U8, align_bytes=64)
+
+        def quantise_head_weights():
+            head_grouped = keep.tile([P, 2, D, PACK], BF16, align_bytes=64)
+            for w in (MEAN, LOGVAR):
+                regroup(nc.vector.tensor_copy, head_grouped[:, w], head_raw[:, w])
+            nc.vector.quantize_mx(
+                out=head_codes[:].rearrange("p w d -> p (w d)").bitcast(FP8X4),
+                scales=head_scales[:].rearrange("p w d -> p (w d)"),
+                in_=head_grouped[:].rearrange("p w d t -> p (w d t)"),
+            )
+
+        en1_codes = keep.tile([P, PASSES1, ROWS], U32, align_bytes=64)
+        en1_scales = keep.tile([P, PASSES1, ROWS], U8, align_bytes=64)
+        en2_codes = keep.tile([P, ROWS], U32, align_bytes=64)
+        en2_scales = keep.tile([P, ROWS], U8, align_bytes=64)
+        stats = keep.tile([P, 3, BANKS, BN_STATS_DIM], F32)
+        head_out = {}
+
+        def flip_and_quantise_en1(s):
+            en1_grouped = stage_pool.tile([P, PASSES1, STAGE, PACK], BF16, align_bytes=64)
+            for i in range(CHUNKS_PER_STAGE):
+                words = en1_sb[:, s * CHUNKS_PER_STAGE + i, :].bitcast(F32)
+                flipped = psum_flip.tile([P, PASSES1, HALVES, P], F32, tag="flip")
+                for g in range(PASSES1):
+                    for u in range(HALVES):
+                        words_u = words[:, g * HALVES * P + u : (g + 1) * HALVES * P : HALVES]
+                        nc.tensor.transpose(flipped[:, g, u, :], words_u, ident_f32[:])
+                nc.scalar.copy(
+                    out=en1_grouped[:, :, i * P : (i + 1) * P, :].bitcast(F32),
+                    in_=flipped[:].rearrange("q g u n -> q g n u"),
+                )
+            stage_cols = slice(s * STAGE, (s + 1) * STAGE)
+            for g in range(PASSES1):
+                nc.vector.quantize_mx(
+                    out=en1_codes[:, g, stage_cols].bitcast(FP8X4),
+                    scales=en1_scales[:, g, stage_cols],
+                    in_=en1_grouped[:, g].rearrange("q n t -> q (n t)"),
+                )
+
+        def hidden_layer(s):
+            stage_cols = slice(s * STAGE, (s + 1) * STAGE)
+            en2_planes = stage_pool.tile([P, E_TILES, STAGE], BF16)
+            for t in range(E_TILES):
+                e_cols = slice(t * P, (t + 1) * P)
+                acc = psum_acc.tile([P, STAGE], F32, tag="acc")
+                for g in range(PASSES1):
+                    nc.tensor.matmul_mx(
+                        out=acc[:],
+                        lhsT=w2_codes[:, g, e_cols].bitcast(FP8X4),
+                        lhsT_scale=w2_scales[:, g, e_cols],
+                        rhs=en1_codes[:, g, stage_cols].bitcast(FP8X4),
+                        rhs_scale=en1_scales[:, g, stage_cols],
+                        start=(g == 0),
+                        stop=(g == PASSES1 - 1),
+                    )
+                nc.scalar.activation(
+                    out=en2_planes[:, t, :], in_=acc[:], func=ACT.Relu, bias=b2_col[:, t : t + 1], scale=1.0
+                )
+            en2_grouped = stage_pool.tile([P, STAGE, PACK], BF16, align_bytes=64)
+            regroup(nc.vector.tensor_copy, en2_grouped[:], en2_planes[:])
+            nc.vector.quantize_mx(
+                out=en2_codes[:, stage_cols].bitcast(FP8X4),
+                scales=en2_scales[:, stage_cols],
+                in_=en2_grouped[:].rearrange("p n t -> p (n t)"),
+            )
+
+        def heads(s):
+            stage_cols = slice(s * STAGE, (s + 1) * STAGE)
+            b, part = divmod(s, STAGES_PER_BANK)
+            for w in (MEAN, LOGVAR):
+                nc.tensor.matmul_mx(
+                    out=head_out[(w, b)][:, part * STAGE : (part + 1) * STAGE],
+                    lhsT=head_codes[:, w, :].bitcast(FP8X4),
+                    lhsT_scale=head_scales[:, w, :],
+                    rhs=en2_codes[:, stage_cols].bitcast(FP8X4),
+                    rhs_scale=en2_scales[:, stage_cols],
+                    start=True,
+                    stop=True,
+                )
+            if part == STAGES_PER_BANK - 1:
+                nc.vector.bn_stats(out=stats[:, LOGVAR, b, :], in_=head_out[(LOGVAR, b)][:])
+
+        flip_and_quantise_en1(0)
+        b2_col = keep.tile([P, E_TILES], F32)
+        nc.vector.tensor_copy(out=b2_col[:], in_=b2_raw[:])
+        flip_and_quantise_en1(1)
+        quantise_head_weights()
+        hidden_layer(0)
+        flip_and_quantise_en1(2)
+        hidden_layer(1)
+        flip_and_quantise_en1(3)
+        for b in range(BANKS):
+            for w in (MEAN, LOGVAR):
+                head_out[(w, b)] = psum_flip.tile([P, BANK], F32, name="head_out%d%d" % (w, b), tag="flip")
+        heads(0)
+        hidden_layer(2)
+        heads(1)
+        hidden_layer(3)
+        heads(2)
+        eps_flipped = psum_acc.tile([P, CHUNKS, P], BF16, tag="acc")
+        for c in range(CHUNKS):
+            nc.tensor.transpose(eps_flipped[:, c, :], eps_sb[:, c, :], ident_bf16[:])
+        heads(3)
+
+        def mean_and_inverse_std(which, stats, epsilon, factor):
+            mean_var = keep.tile([P, 2], F32, name="mean_var%d" % which)
+            nc.vector.bn_aggr(out=mean_var[:], in_=stats.rearrange("p b s -> p (b s)"))
+            shifted = keep.tile([P, 1], F32, name="shifted%d" % which)
+            nc.vector.tensor_scalar(
+                out=shifted[:], in0=mean_var[:, 1:2], scalar1=epsilon, scalar2=factor, op0=ALU.add, op1=ALU.mult
+            )
+            inv = keep.tile([P, 1], F32, name="inv%d" % which)
+            nc.gpsimd.tensor_tensor(out=inv[:], in0=shifted[:], in1=minus_half[:], op=ALU.pow)
+            return mean_var, shifted, inv
+
+        def store_rows(values_t, b, copy, out):
+            back = psum_acc.tile([P, CHUNKS_PER_BANK, D], F32, tag="acc")
+            for i in range(CHUNKS_PER_BANK):
+                first = (b * CHUNKS_PER_BANK + i) * P
+                nc.tensor.transpose(back[:, i, :], values_t[:, first : first + P], ident_f32[:])
+            rows = rows_pool.tile([P, CHUNKS_PER_BANK, D], F32)
+            copy(out=rows[:], in_=back[:])
+            chunks = slice(b * CHUNKS_PER_BANK, (b + 1) * CHUNKS_PER_BANK)
+            nc.sync.dma_start(out=out.rearrange("(p c) d -> p c d", c=CHUNKS)[:, chunks, :], in_=rows[:])
+
+        noise_t = keep.tile([P, ROWS], F32)
+        y_t = keep.tile([P, ROWS], F32)
+        z_t = keep.tile([P, ROWS], F32)
+        zx_t = keep.tile([P, ROWS], F32)
+        bank_cols = [slice(b * BANK, (b + 1) * BANK) for b in range(BANKS)]
+
+        lv_mean_var, lv_shifted, lv_half_inv = mean_and_inverse_std(LOGVAR, stats[:, LOGVAR], BN_EPS, 4.0)
+        lv_minus_mean = keep.tile([P, 1], F32)
+        nc.vector.tensor_scalar_mul(out=lv_minus_mean[:], in0=lv_mean_var[:, 0:1], scalar1=-1.0)
+        exp_bias = keep.tile([P, 1], F32)
+        nc.scalar.activation(out=exp_bias[:], in_=lv_minus_mean[:], func=ACT.Copy, scale=lv_half_inv[:])
+        for b in range(BANKS):
+            nc.scalar.activation(
+                out=noise_t[:, bank_cols[b]],
+                in_=head_out[(LOGVAR, b)][:],
+                func=ACT.Exp,
+                bias=exp_bias[:],
+                scale=lv_half_inv[:],
+            )
+
+        for b in range(BANKS):
+            nc.vector.bn_stats(out=stats[:, MEAN, b, :], in_=head_out[(MEAN, b)][:])
+        m_mean_var, m_shifted, m_inv = mean_and_inverse_std(MEAN, stats[:, MEAN], BN_EPS, 1.0)
+        for b in range(BANKS):
+            chunks = slice(b * CHUNKS_PER_BANK, (b + 1) * CHUNKS_PER_BANK)
+            nc.vector.tensor_tensor(
+                out=noise_t[:, bank_cols[b]],
+                in0=noise_t[:, bank_cols[b]],
+                in1=eps_flipped[:, chunks, :].rearrange("d c n -> d (c n)"),
+                op=ALU.mult,
+            )
+        m_sd = keep.tile([P, 1], F32)
+        nc.vector.tensor_tensor(out=m_sd[:], in0=m_shifted[:], in1=m_inv[:], op=ALU.mult)
+        y_epsilon = keep.tile([P, 1], F32)
+        nc.vector.tensor_scalar_mul(out=y_epsilon[:], in0=m_shifted[:], scalar1=BN_EPS)
+        z_bias = keep.tile([P, 1], F32)
+        nc.vector.scalar_tensor_tensor(
+            out=z_bias[:], in0=m_mean_var[:, 0:1], scalar=-1.0, in1=m_inv[:], op0=ALU.mult, op1=ALU.mult
+        )
+        for b in range(BANKS):
+            nc.vector.scalar_tensor_tensor(
+                out=y_t[:, bank_cols[b]],
+                in0=noise_t[:, bank_cols[b]],
+                scalar=m_sd[:],
+                in1=head_out[(MEAN, b)][:],
+                op0=ALU.mult,
+                op1=ALU.add,
+            )
+            nc.vector.bn_stats(out=stats[:, SAMPLE, b, :], in_=y_t[:, bank_cols[b]])
+            nc.scalar.activation(
+                out=z_t[:, bank_cols[b]], in_=y_t[:, bank_cols[b]], func=ACT.Identity, bias=z_bias[:], scale=m_inv[:]
+            )
+            store_rows(z_t, b, nc.scalar.copy, out_0)
+
+        y_mean_var, y_shifted, y_inv = mean_and_inverse_std(SAMPLE, stats[:, SAMPLE], y_epsilon[:], 1.0)
+        for b in range(BANKS):
+            nc.vector.tensor_scalar(
+                out=zx_t[:, bank_cols[b]],
+                in0=y_t[:, bank_cols[b]],
+                scalar1=y_mean_var[:, 0:1],
+                scalar2=y_inv[:],
+                op0=ALU.subtract,
+                op1=ALU.mult,
+            )
+        store_rows(zx_t, 0, nc.scalar.copy, out_1)
+        store_rows(zx_t, 1, nc.vector.tensor_copy, out_1)

@@ -19,13 +19,9 @@ ROWS, EN1, EN2, D = 1024, 1024, 512, 128
 BN_EPS = 1e-5
 
 CHUNKS = ROWS // P
-BANK = 512
-BANKS = ROWS // BANK
-CHUNKS_PER_BANK = BANK // P
 STAGE = 256
 STAGES = ROWS // STAGE
 CHUNKS_PER_STAGE = STAGE // P
-STAGES_PER_BANK = BANK // STAGE
 PASSES1 = EN1 // K_PASS
 E_TILES = EN2 // P
 HALVES = 2
@@ -50,7 +46,7 @@ def tile_modelvd_pa_kernel(tc, en1, W2, b2, Wmean, Wlogvar, eps, out_0, out_1):
         ctx.enter_context(tc.manual_schedule())
         keep = ctx.enter_context(tc.tile_pool(name="keep", bufs=1))
         stage_pool = ctx.enter_context(tc.tile_pool(name="stage_pool", bufs=2))
-        rows_pool = ctx.enter_context(tc.tile_pool(name="rows_pool", bufs=2 * BANKS))
+        rows_pool = ctx.enter_context(tc.tile_pool(name="rows_pool", bufs=2 * STAGES))
         psum_flip = ctx.enter_context(tc.psum_pool(name="psum_flip", bufs=4))
         psum_acc = ctx.enter_context(tc.psum_pool(name="psum_acc", bufs=4))
 
@@ -121,7 +117,7 @@ def tile_modelvd_pa_kernel(tc, en1, W2, b2, Wmean, Wlogvar, eps, out_0, out_1):
         en1_scales = keep.tile([P, PASSES1, ROWS], U8, align_bytes=64)
         en2_codes = keep.tile([P, ROWS], U32, align_bytes=64)
         en2_scales = keep.tile([P, ROWS], U8, align_bytes=64)
-        stats = keep.tile([P, 3, BANKS, BN_STATS_DIM], F32)
+        stats = keep.tile([P, 3, STAGES, BN_STATS_DIM], F32)
         head_out = {}
 
         def flip_and_quantise_en1(s):
@@ -145,6 +141,8 @@ def tile_modelvd_pa_kernel(tc, en1, W2, b2, Wmean, Wlogvar, eps, out_0, out_1):
                     in_=en1_grouped[:, g].rearrange("q n t -> q (n t)"),
                 )
 
+        en2_grouped = {}
+
         def hidden_layer(s):
             stage_cols = slice(s * STAGE, (s + 1) * STAGE)
             en2_planes = stage_pool.tile([P, E_TILES, STAGE], BF16)
@@ -164,20 +162,23 @@ def tile_modelvd_pa_kernel(tc, en1, W2, b2, Wmean, Wlogvar, eps, out_0, out_1):
                 nc.scalar.activation(
                     out=en2_planes[:, t, :], in_=acc[:], func=ACT.Relu, bias=b2_col[:, t : t + 1], scale=1.0
                 )
-            en2_grouped = stage_pool.tile([P, STAGE, PACK], BF16, align_bytes=64)
-            regroup(nc.vector.tensor_copy, en2_grouped[:], en2_planes[:])
+            en2_grouped[s] = stage_pool.tile([P, STAGE, PACK], BF16, name="en2_grouped%d" % s, tag="en2_grouped", align_bytes=64)
+            regroup(nc.vector.tensor_copy, en2_grouped[s][:], en2_planes[:])
+
+        def quantise_en2(s):
+            stage_cols = slice(s * STAGE, (s + 1) * STAGE)
             nc.vector.quantize_mx(
                 out=en2_codes[:, stage_cols].bitcast(FP8X4),
                 scales=en2_scales[:, stage_cols],
-                in_=en2_grouped[:].rearrange("p n t -> p (n t)"),
+                in_=en2_grouped[s][:].rearrange("p n t -> p (n t)"),
             )
 
         def heads(s):
             stage_cols = slice(s * STAGE, (s + 1) * STAGE)
-            b, part = divmod(s, STAGES_PER_BANK)
-            for w in (MEAN, LOGVAR):
+            head_out[s] = psum_flip.tile([P, 2, STAGE], F32, name="head_out%d" % s, tag="flip")
+            for w in (LOGVAR, MEAN):
                 nc.tensor.matmul_mx(
-                    out=head_out[(w, b)][:, part * STAGE : (part + 1) * STAGE],
+                    out=head_out[s][:, w, :],
                     lhsT=head_codes[:, w, :].bitcast(FP8X4),
                     lhsT_scale=head_scales[:, w, :],
                     rhs=en2_codes[:, stage_cols].bitcast(FP8X4),
@@ -185,8 +186,9 @@ def tile_modelvd_pa_kernel(tc, en1, W2, b2, Wmean, Wlogvar, eps, out_0, out_1):
                     start=True,
                     stop=True,
                 )
-            if part == STAGES_PER_BANK - 1:
-                nc.vector.bn_stats(out=stats[:, LOGVAR, b, :], in_=head_out[(LOGVAR, b)][:])
+
+        def head_stats(s, w):
+            nc.vector.bn_stats(out=stats[:, w, s, :], in_=head_out[s][:, w, :])
 
         flip_and_quantise_en1(0)
         b2_col = keep.tile([P, E_TILES], F32)
@@ -194,106 +196,127 @@ def tile_modelvd_pa_kernel(tc, en1, W2, b2, Wmean, Wlogvar, eps, out_0, out_1):
         flip_and_quantise_en1(1)
         quantise_head_weights()
         hidden_layer(0)
+        quantise_en2(0)
         flip_and_quantise_en1(2)
         hidden_layer(1)
+        quantise_en2(1)
         flip_and_quantise_en1(3)
-        for b in range(BANKS):
-            for w in (MEAN, LOGVAR):
-                head_out[(w, b)] = psum_flip.tile([P, BANK], F32, name="head_out%d%d" % (w, b), tag="flip")
         heads(0)
         hidden_layer(2)
+        quantise_en2(2)
         heads(1)
+        for s in (0, 1):
+            for w in (LOGVAR, MEAN):
+                head_stats(s, w)
         hidden_layer(3)
         heads(2)
         eps_flipped = psum_acc.tile([P, CHUNKS, P], BF16, tag="acc")
         for c in range(CHUNKS):
             nc.tensor.transpose(eps_flipped[:, c, :], eps_sb[:, c, :], ident_bf16[:])
+        head_stats(2, LOGVAR)
+        quantise_en2(3)
         heads(3)
+        head_stats(2, MEAN)
+        head_stats(3, LOGVAR)
+        head_stats(3, MEAN)
 
-        def mean_and_inverse_std(which, stats, epsilon, factor):
-            mean_var = keep.tile([P, 2], F32, name="mean_var%d" % which)
-            nc.vector.bn_aggr(out=mean_var[:], in_=stats.rearrange("p b s -> p (b s)"))
-            shifted = keep.tile([P, 1], F32, name="shifted%d" % which)
+        lv_mean_var = keep.tile([P, 2], F32)
+        lv_shifted = keep.tile([P, 1], F32)
+        lv_half_inv = keep.tile([P, 1], F32)
+        lv_minus_mean = keep.tile([P, 1], F32)
+        lv_bias = keep.tile([P, 1], F32)
+        m_mean_var = keep.tile([P, 2], F32)
+        m_shifted = keep.tile([P, 1], F32)
+        m_inv = keep.tile([P, 1], F32)
+        m_minus_mean = keep.tile([P, 1], F32)
+        m_bias = keep.tile([P, 1], F32)
+        z_mean_var = keep.tile([P, 2], F32)
+        z_shifted = keep.tile([P, 1], F32)
+        z_inv = keep.tile([P, 1], F32)
+
+        def aggregate(mean_var, w):
+            nc.vector.bn_aggr(out=mean_var[:], in_=stats[:, w].rearrange("p s f -> p (s f)"))
+
+        def shift(shifted, mean_var, factor):
             nc.vector.tensor_scalar(
-                out=shifted[:], in0=mean_var[:, 1:2], scalar1=epsilon, scalar2=factor, op0=ALU.add, op1=ALU.mult
+                out=shifted[:], in0=mean_var[:, 1:2], scalar1=BN_EPS, scalar2=factor, op0=ALU.add, op1=ALU.mult
             )
-            inv = keep.tile([P, 1], F32, name="inv%d" % which)
-            nc.gpsimd.tensor_tensor(out=inv[:], in0=shifted[:], in1=minus_half[:], op=ALU.pow)
-            return mean_var, shifted, inv
 
-        def store_rows(values_t, b, copy, out):
-            back = psum_acc.tile([P, CHUNKS_PER_BANK, D], F32, tag="acc")
-            for i in range(CHUNKS_PER_BANK):
-                first = (b * CHUNKS_PER_BANK + i) * P
-                nc.tensor.transpose(back[:, i, :], values_t[:, first : first + P], ident_f32[:])
-            rows = rows_pool.tile([P, CHUNKS_PER_BANK, D], F32)
-            copy(out=rows[:], in_=back[:])
-            chunks = slice(b * CHUNKS_PER_BANK, (b + 1) * CHUNKS_PER_BANK)
-            nc.sync.dma_start(out=out.rearrange("(p c) d -> p c d", c=CHUNKS)[:, chunks, :], in_=rows[:])
+        def inverse_sqrt(inv, shifted):
+            nc.gpsimd.tensor_tensor(out=inv[:], in0=shifted[:], in1=minus_half[:], op=ALU.pow)
+
+        aggregate(lv_mean_var, LOGVAR)
+        aggregate(m_mean_var, MEAN)
+        shift(lv_shifted, lv_mean_var, 4.0)
+        inverse_sqrt(lv_half_inv, lv_shifted)
+        shift(m_shifted, m_mean_var, 1.0)
+        inverse_sqrt(m_inv, m_shifted)
+        nc.vector.tensor_scalar_mul(out=lv_minus_mean[:], in0=lv_mean_var[:, 0:1], scalar1=-1.0)
+        nc.vector.tensor_scalar_mul(out=m_minus_mean[:], in0=m_mean_var[:, 0:1], scalar1=-1.0)
+        nc.scalar.activation(out=lv_bias[:], in_=lv_minus_mean[:], func=ACT.Copy, scale=lv_half_inv[:])
+        nc.gpsimd.tensor_tensor(out=m_bias[:], in0=m_minus_mean[:], in1=m_inv[:], op=ALU.mult)
 
         noise_t = keep.tile([P, ROWS], F32)
-        y_t = keep.tile([P, ROWS], F32)
+        m_t = keep.tile([P, ROWS], F32)
         z_t = keep.tile([P, ROWS], F32)
         zx_t = keep.tile([P, ROWS], F32)
-        bank_cols = [slice(b * BANK, (b + 1) * BANK) for b in range(BANKS)]
+        cols = [slice(s * STAGE, (s + 1) * STAGE) for s in range(STAGES)]
+        chunks = [slice(s * CHUNKS_PER_STAGE, (s + 1) * CHUNKS_PER_STAGE) for s in range(STAGES)]
 
-        lv_mean_var, lv_shifted, lv_half_inv = mean_and_inverse_std(LOGVAR, stats[:, LOGVAR], BN_EPS, 4.0)
-        lv_minus_mean = keep.tile([P, 1], F32)
-        nc.vector.tensor_scalar_mul(out=lv_minus_mean[:], in0=lv_mean_var[:, 0:1], scalar1=-1.0)
-        exp_bias = keep.tile([P, 1], F32)
-        nc.scalar.activation(out=exp_bias[:], in_=lv_minus_mean[:], func=ACT.Copy, scale=lv_half_inv[:])
-        for b in range(BANKS):
+        for s in range(STAGES):
             nc.scalar.activation(
-                out=noise_t[:, bank_cols[b]],
-                in_=head_out[(LOGVAR, b)][:],
+                out=noise_t[:, cols[s]],
+                in_=head_out[s][:, LOGVAR, :],
                 func=ACT.Exp,
-                bias=exp_bias[:],
+                bias=lv_bias[:],
                 scale=lv_half_inv[:],
             )
-
-        for b in range(BANKS):
-            nc.vector.bn_stats(out=stats[:, MEAN, b, :], in_=head_out[(MEAN, b)][:])
-        m_mean_var, m_shifted, m_inv = mean_and_inverse_std(MEAN, stats[:, MEAN], BN_EPS, 1.0)
-        for b in range(BANKS):
-            chunks = slice(b * CHUNKS_PER_BANK, (b + 1) * CHUNKS_PER_BANK)
+        for s in range(STAGES):
+            nc.scalar.activation(
+                out=m_t[:, cols[s]], in_=head_out[s][:, MEAN, :], func=ACT.Identity, bias=m_bias[:], scale=m_inv[:]
+            )
+        for s in range(STAGES):
             nc.vector.tensor_tensor(
-                out=noise_t[:, bank_cols[b]],
-                in0=noise_t[:, bank_cols[b]],
-                in1=eps_flipped[:, chunks, :].rearrange("d c n -> d (c n)"),
+                out=noise_t[:, cols[s]],
+                in0=noise_t[:, cols[s]],
+                in1=eps_flipped[:, chunks[s], :].rearrange("d c n -> d (c n)"),
                 op=ALU.mult,
             )
-        m_sd = keep.tile([P, 1], F32)
-        nc.vector.tensor_tensor(out=m_sd[:], in0=m_shifted[:], in1=m_inv[:], op=ALU.mult)
-        y_epsilon = keep.tile([P, 1], F32)
-        nc.vector.tensor_scalar_mul(out=y_epsilon[:], in0=m_shifted[:], scalar1=BN_EPS)
-        z_bias = keep.tile([P, 1], F32)
-        nc.vector.scalar_tensor_tensor(
-            out=z_bias[:], in0=m_mean_var[:, 0:1], scalar=-1.0, in1=m_inv[:], op0=ALU.mult, op1=ALU.mult
-        )
-        for b in range(BANKS):
-            nc.vector.scalar_tensor_tensor(
-                out=y_t[:, bank_cols[b]],
-                in0=noise_t[:, bank_cols[b]],
-                scalar=m_sd[:],
-                in1=head_out[(MEAN, b)][:],
-                op0=ALU.mult,
-                op1=ALU.add,
-            )
-            nc.vector.bn_stats(out=stats[:, SAMPLE, b, :], in_=y_t[:, bank_cols[b]])
-            nc.scalar.activation(
-                out=z_t[:, bank_cols[b]], in_=y_t[:, bank_cols[b]], func=ACT.Identity, bias=z_bias[:], scale=m_inv[:]
-            )
-            store_rows(z_t, b, nc.scalar.copy, out_0)
 
-        y_mean_var, y_shifted, y_inv = mean_and_inverse_std(SAMPLE, stats[:, SAMPLE], y_epsilon[:], 1.0)
-        for b in range(BANKS):
+        def sample(s):
+            nc.vector.tensor_tensor(out=z_t[:, cols[s]], in0=noise_t[:, cols[s]], in1=m_t[:, cols[s]], op=ALU.add)
+
+        def sample_stats(s):
+            nc.vector.bn_stats(out=stats[:, SAMPLE, s, :], in_=z_t[:, cols[s]])
+
+        sample(0)
+        for s in range(1, STAGES):
+            sample(s)
+            sample_stats(s - 1)
+        sample_stats(STAGES - 1)
+        aggregate(z_mean_var, SAMPLE)
+        shift(z_shifted, z_mean_var, 1.0)
+        inverse_sqrt(z_inv, z_shifted)
+
+        def store_rows(values_t, s, copy, psum, tag, out):
+            back = psum.tile([P, CHUNKS_PER_STAGE, D], F32, tag=tag)
+            for i in range(CHUNKS_PER_STAGE):
+                first = s * STAGE + i * P
+                nc.tensor.transpose(back[:, i, :], values_t[:, first : first + P], ident_f32[:])
+            rows = rows_pool.tile([P, CHUNKS_PER_STAGE, D], F32)
+            copy(out=rows[:], in_=back[:])
+            nc.sync.dma_start(out=out.rearrange("(p c) d -> p c d", c=CHUNKS)[:, chunks[s], :], in_=rows[:])
+
+        for s in range(STAGES):
+            store_rows(z_t, s, nc.scalar.copy, psum_acc, "acc", out_0)
+        for s in range(STAGES):
             nc.vector.tensor_scalar(
-                out=zx_t[:, bank_cols[b]],
-                in0=y_t[:, bank_cols[b]],
-                scalar1=y_mean_var[:, 0:1],
-                scalar2=y_inv[:],
+                out=zx_t[:, cols[s]],
+                in0=z_t[:, cols[s]],
+                scalar1=z_mean_var[:, 0:1],
+                scalar2=z_inv[:],
                 op0=ALU.subtract,
                 op1=ALU.mult,
             )
-        store_rows(zx_t, 0, nc.scalar.copy, out_1)
-        store_rows(zx_t, 1, nc.vector.tensor_copy, out_1)
+        for s in range(STAGES):
+            store_rows(zx_t, s, (nc.scalar.copy, nc.vector.tensor_copy)[s % 2], psum_flip, "flip", out_1)

@@ -24,6 +24,7 @@ STAGES = ROWS // STAGE
 CHUNKS_PER_STAGE = STAGE // P
 PASSES1 = EN1 // K_PASS
 E_TILES = EN2 // P
+W2_SPLIT = 84
 HALVES = 2
 RUN = 4
 
@@ -60,40 +61,45 @@ def tile_modelvd_pa_kernel(tc, en1, W2, b2, Wmean, Wlogvar, eps, out_0, out_1):
         nc.scalar.activation(out=table_warmer[:], in_=minus_half[:], func=ACT.Exp)
 
         w2_raw = keep.tile([P, PASSES1, PACK, EN2], BF16)
-        for g in range(PASSES1):
+
+        def load_w2(g):
             nc.sync.dma_start(
                 out=w2_raw[:, g],
                 in_=W2[g * K_PASS : (g + 1) * K_PASS, :].rearrange("(q j) c -> q j c", j=PACK),
             )
+
         b2_raw = keep.tile([P, E_TILES], BF16)
-        nc.sync.dma_start(out=b2_raw[:], in_=b2.rearrange("(p t) -> p t", t=E_TILES))
         en1_sb = keep.tile([P, CHUNKS, EN1], BF16)
         en1_rows = en1.rearrange("(p c) k -> p c k", c=CHUNKS)
         head_raw = keep.tile([P, 2, PACK, D], BF16)
         eps_sb = keep.tile([P, CHUNKS, D], BF16)
 
-        def load_en1(s):
-            chunks = slice(s * CHUNKS_PER_STAGE, (s + 1) * CHUNKS_PER_STAGE)
-            nc.sync.dma_start(out=en1_sb[:, chunks, :], in_=en1_rows[:, chunks, :])
+        def load_en1(first, last):
+            nc.sync.dma_start(out=en1_sb[:, first:last, :], in_=en1_rows[:, first:last, :])
 
-        load_en1(0)
-        load_en1(1)
+        load_w2(0)
+        load_en1(0, 1)
+        load_en1(1, 2)
+        load_w2(1)
+        nc.sync.dma_start(out=b2_raw[:], in_=b2.rearrange("(p t) -> p t", t=E_TILES))
+        load_en1(2, 4)
         nc.sync.dma_start(out=head_raw[:, MEAN], in_=Wmean.rearrange("(p t) d -> p t d", t=PACK))
         nc.sync.dma_start(out=head_raw[:, LOGVAR], in_=Wlogvar.rearrange("(p t) d -> p t d", t=PACK))
-        load_en1(2)
-        load_en1(3)
+        load_en1(4, 6)
+        load_en1(6, 8)
         nc.sync.dma_start(out=eps_sb[:], in_=eps.rearrange("(p c) d -> p c d", c=CHUNKS))
 
         w2_grouped = keep.tile([P, PASSES1, EN2, PACK], BF16, align_bytes=64)
         w2_codes = keep.tile([P, PASSES1, EN2], U32, align_bytes=64)
         w2_scales = keep.tile([P, PASSES1, EN2], U8, align_bytes=64)
-        for g in range(PASSES1):
+
+        def regroup_w2(g):
             grouped = w2_grouped[:, g].rearrange("q (t m) j -> q m j t", t=E_TILES)
             raw = w2_raw[:, g].rearrange("q j (m t) -> q m j t", t=E_TILES)
-            half = P // 2
-            nc.vector.tensor_copy(out=grouped[:, 0:half], in_=raw[:, 0:half])
-            nc.scalar.copy(out=grouped[:, half:P], in_=raw[:, half:P])
-        for g in range(PASSES1):
+            nc.vector.tensor_copy(out=grouped[:, 0:W2_SPLIT], in_=raw[:, 0:W2_SPLIT])
+            nc.scalar.copy(out=grouped[:, W2_SPLIT:P], in_=raw[:, W2_SPLIT:P])
+
+        def quantise_w2(g):
             nc.vector.quantize_mx(
                 out=w2_codes[:, g, :].bitcast(FP8X4),
                 scales=w2_scales[:, g, :],
@@ -113,15 +119,18 @@ def tile_modelvd_pa_kernel(tc, en1, W2, b2, Wmean, Wlogvar, eps, out_0, out_1):
                 in_=head_grouped[:].rearrange("p w d t -> p (w d t)"),
             )
 
-        en1_codes = keep.tile([P, PASSES1, ROWS], U32, align_bytes=64)
-        en1_scales = keep.tile([P, PASSES1, ROWS], U8, align_bytes=64)
+        en1_codes = keep.tile([P, STAGES, PASSES1, STAGE], U32, align_bytes=64)
+        en1_scales = keep.tile([P, STAGES, PASSES1, STAGE], U8, align_bytes=64)
         en2_codes = keep.tile([P, ROWS], U32, align_bytes=64)
         en2_scales = keep.tile([P, ROWS], U8, align_bytes=64)
+        b2_col = keep.tile([P, E_TILES], F32)
         stats = keep.tile([P, 3, STAGES, BN_STATS_DIM], F32)
-        head_out = {}
+        en1_grouped, acc, en2_planes, en2_grouped, head_out = {}, {}, {}, {}, {}
 
-        def flip_and_quantise_en1(s):
-            en1_grouped = stage_pool.tile([P, PASSES1, STAGE, PACK], BF16, align_bytes=64)
+        def flip_en1(s):
+            en1_grouped[s] = stage_pool.tile(
+                [P, PASSES1, STAGE, PACK], BF16, name="en1_grouped%d" % s, tag="en1_grouped", align_bytes=64
+            )
             for i in range(CHUNKS_PER_STAGE):
                 words = en1_sb[:, s * CHUNKS_PER_STAGE + i, :].bitcast(F32)
                 flipped = psum_flip.tile([P, PASSES1, HALVES, P], F32, tag="flip")
@@ -130,40 +139,42 @@ def tile_modelvd_pa_kernel(tc, en1, W2, b2, Wmean, Wlogvar, eps, out_0, out_1):
                         words_u = words[:, g * HALVES * P + u : (g + 1) * HALVES * P : HALVES]
                         nc.tensor.transpose(flipped[:, g, u, :], words_u, ident_f32[:])
                 nc.scalar.copy(
-                    out=en1_grouped[:, :, i * P : (i + 1) * P, :].bitcast(F32),
+                    out=en1_grouped[s][:, :, i * P : (i + 1) * P, :].bitcast(F32),
                     in_=flipped[:].rearrange("q g u n -> q g n u"),
                 )
-            stage_cols = slice(s * STAGE, (s + 1) * STAGE)
-            for g in range(PASSES1):
-                nc.vector.quantize_mx(
-                    out=en1_codes[:, g, stage_cols].bitcast(FP8X4),
-                    scales=en1_scales[:, g, stage_cols],
-                    in_=en1_grouped[:, g].rearrange("q n t -> q (n t)"),
-                )
 
-        en2_grouped = {}
+        def quantise_en1(s):
+            nc.vector.quantize_mx(
+                out=en1_codes[:, s].rearrange("q g n -> q (g n)").bitcast(FP8X4),
+                scales=en1_scales[:, s].rearrange("q g n -> q (g n)"),
+                in_=en1_grouped[s][:].rearrange("q g n t -> q (g n t)"),
+            )
 
-        def hidden_layer(s):
-            stage_cols = slice(s * STAGE, (s + 1) * STAGE)
-            en2_planes = stage_pool.tile([P, E_TILES, STAGE], BF16)
+        def multiply(s):
             for t in range(E_TILES):
                 e_cols = slice(t * P, (t + 1) * P)
-                acc = psum_acc.tile([P, STAGE], F32, tag="acc")
+                acc[s, t] = psum_acc.tile([P, STAGE], F32, name="acc%d%d" % (s, t), tag="acc")
                 for g in range(PASSES1):
                     nc.tensor.matmul_mx(
-                        out=acc[:],
+                        out=acc[s, t][:],
                         lhsT=w2_codes[:, g, e_cols].bitcast(FP8X4),
                         lhsT_scale=w2_scales[:, g, e_cols],
-                        rhs=en1_codes[:, g, stage_cols].bitcast(FP8X4),
-                        rhs_scale=en1_scales[:, g, stage_cols],
+                        rhs=en1_codes[:, s, g, :].bitcast(FP8X4),
+                        rhs_scale=en1_scales[:, s, g, :],
                         start=(g == 0),
                         stop=(g == PASSES1 - 1),
                     )
+
+        def bias_and_relu(s):
+            en2_planes[s] = stage_pool.tile([P, E_TILES, STAGE], BF16, name="en2_planes%d" % s, tag="en2_planes")
+            for t in range(E_TILES):
                 nc.scalar.activation(
-                    out=en2_planes[:, t, :], in_=acc[:], func=ACT.Relu, bias=b2_col[:, t : t + 1], scale=1.0
+                    out=en2_planes[s][:, t, :], in_=acc[s, t][:], func=ACT.Relu, bias=b2_col[:, t : t + 1], scale=1.0
                 )
+
+        def regroup_en2(s):
             en2_grouped[s] = stage_pool.tile([P, STAGE, PACK], BF16, name="en2_grouped%d" % s, tag="en2_grouped", align_bytes=64)
-            regroup(nc.vector.tensor_copy, en2_grouped[s][:], en2_planes[:])
+            regroup(nc.vector.tensor_copy, en2_grouped[s][:], en2_planes[s][:])
 
         def quantise_en2(s):
             stage_cols = slice(s * STAGE, (s + 1) * STAGE)
@@ -190,35 +201,49 @@ def tile_modelvd_pa_kernel(tc, en1, W2, b2, Wmean, Wlogvar, eps, out_0, out_1):
         def head_stats(s, w):
             nc.vector.bn_stats(out=stats[:, w, s, :], in_=head_out[s][:, w, :])
 
-        flip_and_quantise_en1(0)
-        b2_col = keep.tile([P, E_TILES], F32)
+        regroup_w2(0)
+        quantise_w2(0)
+        flip_en1(0)
+        regroup_w2(1)
+        quantise_en1(0)
+        quantise_w2(1)
         nc.vector.tensor_copy(out=b2_col[:], in_=b2_raw[:])
-        flip_and_quantise_en1(1)
+        flip_en1(1)
+        multiply(0)
         quantise_head_weights()
-        hidden_layer(0)
+        quantise_en1(1)
+        bias_and_relu(0)
+        flip_en1(2)
+        regroup_en2(0)
+        quantise_en1(2)
         quantise_en2(0)
-        flip_and_quantise_en1(2)
-        hidden_layer(1)
-        quantise_en2(1)
-        flip_and_quantise_en1(3)
+        flip_en1(3)
+        multiply(1)
+        bias_and_relu(1)
         heads(0)
-        hidden_layer(2)
-        quantise_en2(2)
+        multiply(2)
+        quantise_en1(3)
+        head_stats(0, LOGVAR)
+        head_stats(0, MEAN)
+        regroup_en2(1)
+        bias_and_relu(2)
+        multiply(3)
+        quantise_en2(1)
         heads(1)
-        for s in (0, 1):
-            for w in (LOGVAR, MEAN):
-                head_stats(s, w)
-        hidden_layer(3)
+        regroup_en2(2)
+        quantise_en2(2)
         heads(2)
+        bias_and_relu(3)
         eps_flipped = psum_acc.tile([P, CHUNKS, P], BF16, tag="acc")
         for c in range(CHUNKS):
             nc.tensor.transpose(eps_flipped[:, c, :], eps_sb[:, c, :], ident_bf16[:])
-        head_stats(2, LOGVAR)
+        regroup_en2(3)
+        head_stats(1, LOGVAR)
         quantise_en2(3)
         heads(3)
-        head_stats(2, MEAN)
+        head_stats(2, LOGVAR)
+        head_stats(1, MEAN)
         head_stats(3, LOGVAR)
-        head_stats(3, MEAN)
 
         lv_mean_var = keep.tile([P, 2], F32)
         lv_shifted = keep.tile([P, 1], F32)
@@ -246,12 +271,14 @@ def tile_modelvd_pa_kernel(tc, en1, W2, b2, Wmean, Wlogvar, eps, out_0, out_1):
             nc.gpsimd.tensor_tensor(out=inv[:], in0=shifted[:], in1=minus_half[:], op=ALU.pow)
 
         aggregate(lv_mean_var, LOGVAR)
-        aggregate(m_mean_var, MEAN)
         shift(lv_shifted, lv_mean_var, 4.0)
         inverse_sqrt(lv_half_inv, lv_shifted)
+        nc.vector.tensor_scalar_mul(out=lv_minus_mean[:], in0=lv_mean_var[:, 0:1], scalar1=-1.0)
+        head_stats(2, MEAN)
+        head_stats(3, MEAN)
+        aggregate(m_mean_var, MEAN)
         shift(m_shifted, m_mean_var, 1.0)
         inverse_sqrt(m_inv, m_shifted)
-        nc.vector.tensor_scalar_mul(out=lv_minus_mean[:], in0=lv_mean_var[:, 0:1], scalar1=-1.0)
         nc.vector.tensor_scalar_mul(out=m_minus_mean[:], in0=m_mean_var[:, 0:1], scalar1=-1.0)
         nc.scalar.activation(out=lv_bias[:], in_=lv_minus_mean[:], func=ACT.Copy, scale=lv_half_inv[:])
         nc.gpsimd.tensor_tensor(out=m_bias[:], in0=m_minus_mean[:], in1=m_inv[:], op=ALU.mult)

@@ -57,6 +57,10 @@ def tile_modelvd_pa_kernel(tc, en1, W2, b2, Wmean, Wlogvar, eps, out_0, out_1):
         make_identity(nc, ident_bf16[:])
         minus_half = keep.tile([P, 1], F32)
         nc.vector.memset(minus_half[:], -0.5)
+        epsilon = keep.tile([P, 1], F32)
+        nc.vector.tensor_scalar(
+            out=epsilon[:], in0=minus_half[:], scalar1=0.0, scalar2=BN_EPS, op0=ALU.mult, op1=ALU.add
+        )
         table_warmer = keep.tile([P, 1], F32)
         nc.scalar.activation(out=table_warmer[:], in_=minus_half[:], func=ACT.Exp)
 
@@ -256,7 +260,6 @@ def tile_modelvd_pa_kernel(tc, en1, W2, b2, Wmean, Wlogvar, eps, out_0, out_1):
         m_minus_mean = keep.tile([P, 1], F32)
         m_bias = keep.tile([P, 1], F32)
         z_mean_var = keep.tile([P, 2], F32)
-        z_shifted = keep.tile([P, 1], F32)
         z_inv = keep.tile([P, 1], F32)
 
         def aggregate(mean_var, w):
@@ -300,7 +303,7 @@ def tile_modelvd_pa_kernel(tc, en1, W2, b2, Wmean, Wlogvar, eps, out_0, out_1):
             )
         for s in range(STAGES):
             nc.scalar.activation(
-                out=m_t[:, cols[s]], in_=head_out[s][:, MEAN, :], func=ACT.Identity, bias=m_bias[:], scale=m_inv[:]
+                out=m_t[:, cols[s]], in_=head_out[s][:, MEAN, :], func=ACT.Copy, scale=m_inv[:]
             )
         for s in range(STAGES):
             nc.vector.tensor_tensor(
@@ -311,7 +314,14 @@ def tile_modelvd_pa_kernel(tc, en1, W2, b2, Wmean, Wlogvar, eps, out_0, out_1):
             )
 
         def sample(s):
-            nc.vector.tensor_tensor(out=z_t[:, cols[s]], in0=noise_t[:, cols[s]], in1=m_t[:, cols[s]], op=ALU.add)
+            nc.vector.scalar_tensor_tensor(
+                out=z_t[:, cols[s]],
+                in0=noise_t[:, cols[s]],
+                scalar=m_bias[:],
+                in1=m_t[:, cols[s]],
+                op0=ALU.add,
+                op1=ALU.add,
+            )
 
         def sample_stats(s):
             nc.vector.bn_stats(out=stats[:, SAMPLE, s, :], in_=z_t[:, cols[s]])
@@ -322,8 +332,6 @@ def tile_modelvd_pa_kernel(tc, en1, W2, b2, Wmean, Wlogvar, eps, out_0, out_1):
             sample_stats(s - 1)
         sample_stats(STAGES - 1)
         aggregate(z_mean_var, SAMPLE)
-        shift(z_shifted, z_mean_var, 1.0)
-        inverse_sqrt(z_inv, z_shifted)
 
         def store_rows(values_t, s, copy, psum, tag, out):
             back = psum.tile([P, CHUNKS_PER_STAGE, D], F32, tag=tag)
@@ -334,7 +342,13 @@ def tile_modelvd_pa_kernel(tc, en1, W2, b2, Wmean, Wlogvar, eps, out_0, out_1):
             copy(out=rows[:], in_=back[:])
             nc.sync.dma_start(out=out.rearrange("(p c) d -> p c d", c=CHUNKS)[:, chunks[s], :], in_=rows[:])
 
-        for s in range(STAGES):
+        nc.scalar.activation(out=table_warmer[:], in_=epsilon[:], func=ACT.Abs_reciprocal_sqrt)
+        store_rows(z_t, 0, nc.scalar.copy, psum_acc, "acc", out_0)
+        nc.scalar.activation(
+            out=z_inv[:], in_=z_mean_var[:, 1:2], func=ACT.Abs_reciprocal_sqrt, bias=epsilon[:], scale=1.0
+        )
+        store_rows(z_t, 1, nc.vector.tensor_copy, psum_acc, "acc", out_0)
+        for s in (2, 3):
             store_rows(z_t, s, nc.scalar.copy, psum_acc, "acc", out_0)
         for s in range(STAGES):
             nc.vector.tensor_scalar(

@@ -28,7 +28,7 @@ W2_SPLIT = 84
 HALVES = 2
 RUN = 4
 
-MEAN, LOGVAR, SAMPLE = 0, 1, 2
+MEAN, LOGVAR = 0, 1
 BN_STATS_DIM = 6
 
 FLOPS = 2 * ROWS * EN1 * EN2 + 2 * 2 * ROWS * EN2 * D
@@ -128,7 +128,7 @@ def tile_modelvd_pa_kernel(tc, en1, W2, b2, Wmean, Wlogvar, eps, out_0, out_1):
         en2_codes = keep.tile([P, ROWS], U32, align_bytes=64)
         en2_scales = keep.tile([P, ROWS], U8, align_bytes=64)
         b2_col = keep.tile([P, E_TILES], F32)
-        stats = keep.tile([P, 3, STAGES, BN_STATS_DIM], F32)
+        stats = keep.tile([P, 2, STAGES, BN_STATS_DIM], F32)
         en1_grouped, acc, en2_planes, en2_grouped, head_out = {}, {}, {}, {}, {}
 
         def flip_en1(s):
@@ -205,6 +205,12 @@ def tile_modelvd_pa_kernel(tc, en1, W2, b2, Wmean, Wlogvar, eps, out_0, out_1):
         def head_stats(s, w):
             nc.vector.bn_stats(out=stats[:, w, s, :], in_=head_out[s][:, w, :])
 
+        def add_epsilon():
+            raised = stats[:, MEAN : LOGVAR + 1, 0, 2]
+            nc.vector.tensor_scalar(
+                out=raised, in0=raised, scalar1=BN_EPS * ROWS, scalar2=None, op0=ALU.add
+            )
+
         regroup_w2(0)
         quantise_w2(0)
         flip_en1(0)
@@ -230,6 +236,7 @@ def tile_modelvd_pa_kernel(tc, en1, W2, b2, Wmean, Wlogvar, eps, out_0, out_1):
         head_stats(0, LOGVAR)
         head_stats(0, MEAN)
         regroup_en2(1)
+        add_epsilon()
         bias_and_relu(2)
         multiply(3)
         quantise_en2(1)
@@ -250,46 +257,44 @@ def tile_modelvd_pa_kernel(tc, en1, W2, b2, Wmean, Wlogvar, eps, out_0, out_1):
         head_stats(3, LOGVAR)
 
         lv_mean_var = keep.tile([P, 2], F32)
-        lv_shifted = keep.tile([P, 1], F32)
+        lv_inv = keep.tile([P, 1], F32)
         lv_half_inv = keep.tile([P, 1], F32)
-        lv_minus_mean = keep.tile([P, 1], F32)
+        lv_minus_half_mean = keep.tile([P, 1], F32)
         lv_bias = keep.tile([P, 1], F32)
         m_mean_var = keep.tile([P, 2], F32)
-        m_shifted = keep.tile([P, 1], F32)
         m_inv = keep.tile([P, 1], F32)
         m_minus_mean = keep.tile([P, 1], F32)
         m_bias = keep.tile([P, 1], F32)
-        z_mean_var = keep.tile([P, 2], F32)
+        noise_sums = keep.tile([P, STAGES], F32)
+        noise_sum = keep.tile([P, 1], F32)
+        centre = keep.tile([P, 1], F32)
+        z_squares = keep.tile([P, 2], F32)
+        z_var_part = keep.tile([P, 1], F32)
         z_inv = keep.tile([P, 1], F32)
 
         def aggregate(mean_var, w):
             nc.vector.bn_aggr(out=mean_var[:], in_=stats[:, w].rearrange("p s f -> p (s f)"))
 
-        def shift(shifted, mean_var, factor):
-            nc.vector.tensor_scalar(
-                out=shifted[:], in0=mean_var[:, 1:2], scalar1=BN_EPS, scalar2=factor, op0=ALU.add, op1=ALU.mult
-            )
-
-        def inverse_sqrt(inv, shifted):
-            nc.gpsimd.tensor_tensor(out=inv[:], in0=shifted[:], in1=minus_half[:], op=ALU.pow)
+        def inverse_sqrt(inv, mean_var):
+            nc.gpsimd.tensor_tensor(out=inv[:], in0=mean_var[:, 1:2], in1=minus_half[:], op=ALU.pow)
 
         aggregate(lv_mean_var, LOGVAR)
-        shift(lv_shifted, lv_mean_var, 4.0)
-        inverse_sqrt(lv_half_inv, lv_shifted)
-        nc.vector.tensor_scalar_mul(out=lv_minus_mean[:], in0=lv_mean_var[:, 0:1], scalar1=-1.0)
+        inverse_sqrt(lv_inv, lv_mean_var)
         head_stats(2, MEAN)
+        nc.vector.tensor_scalar_mul(out=lv_minus_half_mean[:], in0=lv_mean_var[:, 0:1], scalar1=-0.5)
         head_stats(3, MEAN)
+        nc.scalar.activation(out=lv_half_inv[:], in_=lv_inv[:], func=ACT.Copy, scale=0.5)
+        nc.scalar.activation(out=lv_bias[:], in_=lv_minus_half_mean[:], func=ACT.Copy, scale=lv_inv[:])
         aggregate(m_mean_var, MEAN)
-        shift(m_shifted, m_mean_var, 1.0)
-        inverse_sqrt(m_inv, m_shifted)
+        inverse_sqrt(m_inv, m_mean_var)
         nc.vector.tensor_scalar_mul(out=m_minus_mean[:], in0=m_mean_var[:, 0:1], scalar1=-1.0)
-        nc.scalar.activation(out=lv_bias[:], in_=lv_minus_mean[:], func=ACT.Copy, scale=lv_half_inv[:])
         nc.gpsimd.tensor_tensor(out=m_bias[:], in0=m_minus_mean[:], in1=m_inv[:], op=ALU.mult)
 
         noise_t = keep.tile([P, ROWS], F32)
-        m_t = keep.tile([P, ROWS], F32)
+        y_t = keep.tile([P, ROWS], F32)
         z_t = keep.tile([P, ROWS], F32)
         zx_t = keep.tile([P, ROWS], F32)
+        squares = keep.tile([P, ROWS], F32)
         cols = [slice(s * STAGE, (s + 1) * STAGE) for s in range(STAGES)]
         chunks = [slice(s * CHUNKS_PER_STAGE, (s + 1) * CHUNKS_PER_STAGE) for s in range(STAGES)]
 
@@ -301,37 +306,50 @@ def tile_modelvd_pa_kernel(tc, en1, W2, b2, Wmean, Wlogvar, eps, out_0, out_1):
                 bias=lv_bias[:],
                 scale=lv_half_inv[:],
             )
+        nc.scalar.activation(out=table_warmer[:], in_=epsilon[:], func=ACT.Abs_reciprocal_sqrt)
         for s in range(STAGES):
-            nc.scalar.activation(
-                out=m_t[:, cols[s]], in_=head_out[s][:, MEAN, :], func=ACT.Copy, scale=m_inv[:]
-            )
-        for s in range(STAGES):
-            nc.vector.tensor_tensor(
+            nc.vector.scalar_tensor_tensor(
                 out=noise_t[:, cols[s]],
                 in0=noise_t[:, cols[s]],
+                scalar=1.0,
                 in1=eps_flipped[:, chunks[s], :].rearrange("d c n -> d (c n)"),
-                op=ALU.mult,
+                op0=ALU.mult,
+                op1=ALU.mult,
+                accum_out=noise_sums[:, s : s + 1],
             )
-
-        def sample(s):
+        for s in range(STAGES):
             nc.vector.scalar_tensor_tensor(
-                out=z_t[:, cols[s]],
-                in0=noise_t[:, cols[s]],
-                scalar=m_bias[:],
-                in1=m_t[:, cols[s]],
-                op0=ALU.add,
+                out=y_t[:, cols[s]],
+                in0=head_out[s][:, MEAN, :],
+                scalar=m_inv[:],
+                in1=noise_t[:, cols[s]],
+                op0=ALU.mult,
                 op1=ALU.add,
             )
-
-        def sample_stats(s):
-            nc.vector.bn_stats(out=stats[:, SAMPLE, s, :], in_=z_t[:, cols[s]])
-
-        sample(0)
-        for s in range(1, STAGES):
-            sample(s)
-            sample_stats(s - 1)
-        sample_stats(STAGES - 1)
-        aggregate(z_mean_var, SAMPLE)
+            if s == 0:
+                nc.vector.tensor_reduce(out=noise_sum[:], in_=noise_sums[:], op=ALU.add, axis=mybir.AxisListType.X)
+            if s == 1:
+                nc.vector.scalar_tensor_tensor(
+                    out=centre[:], in0=noise_sum[:], scalar=-1.0 / ROWS, in1=m_bias[:], op0=ALU.mult, op1=ALU.add
+                )
+        for h in range(2):
+            half = slice(h * ROWS // 2, (h + 1) * ROWS // 2)
+            nc.scalar.activation(
+                out=squares[:, half],
+                in_=y_t[:, half],
+                func=ACT.Square,
+                bias=centre[:],
+                scale=1.0,
+                accum_out=z_squares[:, h : h + 1],
+            )
+        for s in range(STAGES):
+            nc.vector.tensor_scalar(out=z_t[:, cols[s]], in0=y_t[:, cols[s]], scalar1=m_bias[:], scalar2=None, op0=ALU.add)
+        nc.vector.tensor_scalar(
+            out=z_var_part[:], in0=z_squares[:, 0:1], scalar1=1.0 / ROWS, scalar2=BN_EPS, op0=ALU.mult, op1=ALU.add
+        )
+        nc.scalar.activation(
+            out=z_inv[:], in_=z_squares[:, 1:2], func=ACT.Abs_reciprocal_sqrt, bias=z_var_part[:], scale=1.0 / ROWS
+        )
 
         def store_rows(values_t, s, copy, psum, tag, out):
             back = psum.tile([P, CHUNKS_PER_STAGE, D], F32, tag=tag)
@@ -342,22 +360,17 @@ def tile_modelvd_pa_kernel(tc, en1, W2, b2, Wmean, Wlogvar, eps, out_0, out_1):
             copy(out=rows[:], in_=back[:])
             nc.sync.dma_start(out=out.rearrange("(p c) d -> p c d", c=CHUNKS)[:, chunks[s], :], in_=rows[:])
 
-        nc.scalar.activation(out=table_warmer[:], in_=epsilon[:], func=ACT.Abs_reciprocal_sqrt)
-        store_rows(z_t, 0, nc.scalar.copy, psum_acc, "acc", out_0)
-        nc.scalar.activation(
-            out=z_inv[:], in_=z_mean_var[:, 1:2], func=ACT.Abs_reciprocal_sqrt, bias=epsilon[:], scale=1.0
-        )
-        store_rows(z_t, 1, nc.vector.tensor_copy, psum_acc, "acc", out_0)
-        for s in (2, 3):
+        for s in range(STAGES - 1):
             store_rows(z_t, s, nc.scalar.copy, psum_acc, "acc", out_0)
         for s in range(STAGES):
             nc.vector.tensor_scalar(
                 out=zx_t[:, cols[s]],
-                in0=z_t[:, cols[s]],
-                scalar1=z_mean_var[:, 0:1],
+                in0=y_t[:, cols[s]],
+                scalar1=centre[:],
                 scalar2=z_inv[:],
-                op0=ALU.subtract,
+                op0=ALU.add,
                 op1=ALU.mult,
             )
+        store_rows(z_t, STAGES - 1, nc.vector.tensor_copy, psum_acc, "acc", out_0)
         for s in range(STAGES):
             store_rows(zx_t, s, (nc.scalar.copy, nc.vector.tensor_copy)[s % 2], psum_flip, "flip", out_1)

@@ -47,7 +47,6 @@ def tile_modelvd_pa_kernel(tc, en1, W2, b2, Wmean, Wlogvar, eps, out_0, out_1):
         ctx.enter_context(tc.manual_schedule())
         keep = ctx.enter_context(tc.tile_pool(name="keep", bufs=1))
         stage_pool = ctx.enter_context(tc.tile_pool(name="stage_pool", bufs=2))
-        rows_pool = ctx.enter_context(tc.tile_pool(name="rows_pool", bufs=2 * STAGES))
         psum_flip = ctx.enter_context(tc.psum_pool(name="psum_flip", bufs=4))
         psum_acc = ctx.enter_context(tc.psum_pool(name="psum_acc", bufs=4))
 
@@ -154,46 +153,54 @@ def tile_modelvd_pa_kernel(tc, en1, W2, b2, Wmean, Wlogvar, eps, out_0, out_1):
                 in_=en1_grouped[s][:].rearrange("q g n t -> q (g n t)"),
             )
 
-        def multiply(s):
+        def multiply(s, rows=(0, STAGE)):
+            first, last = rows
             for t in range(E_TILES):
                 e_cols = slice(t * P, (t + 1) * P)
-                acc[s, t] = psum_acc.tile([P, STAGE], F32, name="acc%d%d" % (s, t), tag="acc")
+                acc[s, t] = psum_acc.tile([P, last - first], F32, name="acc%d%d" % (s, t), tag="acc")
                 for g in range(PASSES1):
                     nc.tensor.matmul_mx(
                         out=acc[s, t][:],
                         lhsT=w2_codes[:, g, e_cols].bitcast(FP8X4),
                         lhsT_scale=w2_scales[:, g, e_cols],
-                        rhs=en1_codes[:, s, g, :].bitcast(FP8X4),
-                        rhs_scale=en1_scales[:, s, g, :],
+                        rhs=en1_codes[:, s, g, first:last].bitcast(FP8X4),
+                        rhs_scale=en1_scales[:, s, g, first:last],
                         start=(g == 0),
                         stop=(g == PASSES1 - 1),
                     )
 
-        def bias_and_relu(s):
-            en2_planes[s] = stage_pool.tile([P, E_TILES, STAGE], BF16, name="en2_planes%d" % s, tag="en2_planes")
+        def bias_and_relu(s, rows=(0, STAGE)):
+            first, last = rows
+            if first == 0:
+                en2_planes[s] = stage_pool.tile([P, E_TILES, STAGE], BF16, name="en2_planes%d" % s, tag="en2_planes")
             for t in range(E_TILES):
                 nc.scalar.activation(
-                    out=en2_planes[s][:, t, :], in_=acc[s, t][:], func=ACT.Relu, bias=b2_col[:, t : t + 1], scale=1.0
+                    out=en2_planes[s][:, t, first:last], in_=acc[s, t][:], func=ACT.Relu, bias=b2_col[:, t : t + 1], scale=1.0
                 )
 
-        def regroup_en2(s):
-            en2_grouped[s] = stage_pool.tile([P, STAGE, PACK], BF16, name="en2_grouped%d" % s, tag="en2_grouped", align_bytes=64)
-            regroup(nc.vector.tensor_copy, en2_grouped[s][:], en2_planes[s][:])
+        def regroup_en2(s, rows=(0, STAGE)):
+            first, last = rows
+            if first == 0:
+                en2_grouped[s] = stage_pool.tile([P, STAGE, PACK], BF16, name="en2_grouped%d" % s, tag="en2_grouped", align_bytes=64)
+            regroup(nc.vector.tensor_copy, en2_grouped[s][:, first:last, :], en2_planes[s][:, :, first:last])
 
-        def quantise_en2(s):
-            stage_cols = slice(s * STAGE, (s + 1) * STAGE)
+        def quantise_en2(s, rows=(0, STAGE)):
+            first, last = rows
+            stage_cols = slice(s * STAGE + first, s * STAGE + last)
             nc.vector.quantize_mx(
                 out=en2_codes[:, stage_cols].bitcast(FP8X4),
                 scales=en2_scales[:, stage_cols],
-                in_=en2_grouped[s][:].rearrange("p n t -> p (n t)"),
+                in_=en2_grouped[s][:, first:last, :].rearrange("p n t -> p (n t)"),
             )
 
-        def heads(s):
-            stage_cols = slice(s * STAGE, (s + 1) * STAGE)
-            head_out[s] = psum_flip.tile([P, 2, STAGE], F32, name="head_out%d" % s, tag="flip")
+        def heads(s, rows=(0, STAGE)):
+            first, last = rows
+            stage_cols = slice(s * STAGE + first, s * STAGE + last)
+            if first == 0:
+                head_out[s] = psum_flip.tile([P, 2, STAGE], F32, name="head_out%d" % s, tag="flip")
             for w in (LOGVAR, MEAN):
                 nc.tensor.matmul_mx(
-                    out=head_out[s][:, w, :],
+                    out=head_out[s][:, w, first:last],
                     lhsT=head_codes[:, w, :].bitcast(FP8X4),
                     lhsT_scale=head_scales[:, w, :],
                     rhs=en2_codes[:, stage_cols].bitcast(FP8X4),
@@ -238,22 +245,26 @@ def tile_modelvd_pa_kernel(tc, en1, W2, b2, Wmean, Wlogvar, eps, out_0, out_1):
         regroup_en2(1)
         add_epsilon()
         bias_and_relu(2)
-        multiply(3)
+        multiply(3, (0, P))
+        bias_and_relu(3, (0, P))
+        multiply(3, (P, STAGE))
+        bias_and_relu(3, (P, STAGE))
         quantise_en2(1)
         heads(1)
-        regroup_en2(2)
-        quantise_en2(2)
-        heads(2)
-        bias_and_relu(3)
         eps_flipped = psum_acc.tile([P, CHUNKS, P], BF16, tag="acc")
         for c in range(CHUNKS):
             nc.tensor.transpose(eps_flipped[:, c, :], eps_sb[:, c, :], ident_bf16[:])
-        regroup_en2(3)
+        regroup_en2(2)
+        quantise_en2(2)
+        heads(2)
+        regroup_en2(3, (0, P))
+        regroup_en2(3, (P, STAGE))
+        quantise_en2(3, (0, P))
+        quantise_en2(3, (P, STAGE))
+        heads(3, (0, P))
+        heads(3, (P, STAGE))
         head_stats(1, LOGVAR)
-        quantise_en2(3)
-        heads(3)
         head_stats(2, LOGVAR)
-        head_stats(1, MEAN)
         head_stats(3, LOGVAR)
 
         lv_mean_var = keep.tile([P, 2], F32)
@@ -280,6 +291,7 @@ def tile_modelvd_pa_kernel(tc, en1, W2, b2, Wmean, Wlogvar, eps, out_0, out_1):
 
         aggregate(lv_mean_var, LOGVAR)
         inverse_sqrt(lv_inv, lv_mean_var)
+        head_stats(1, MEAN)
         head_stats(2, MEAN)
         nc.vector.tensor_scalar_mul(out=lv_minus_half_mean[:], in0=lv_mean_var[:, 0:1], scalar1=-0.5)
         head_stats(3, MEAN)
@@ -351,17 +363,26 @@ def tile_modelvd_pa_kernel(tc, en1, W2, b2, Wmean, Wlogvar, eps, out_0, out_1):
             out=z_inv[:], in_=z_squares[:, 1:2], func=ACT.Abs_reciprocal_sqrt, bias=z_var_part[:], scale=1.0 / ROWS
         )
 
-        def store_rows(values_t, s, copy, psum, tag, out):
+        def back_to_rows(values_t, s, copy, psum, tag, rows):
             back = psum.tile([P, CHUNKS_PER_STAGE, D], F32, tag=tag)
             for i in range(CHUNKS_PER_STAGE):
                 first = s * STAGE + i * P
                 nc.tensor.transpose(back[:, i, :], values_t[:, first : first + P], ident_f32[:])
-            rows = rows_pool.tile([P, CHUNKS_PER_STAGE, D], F32)
-            copy(out=rows[:], in_=back[:])
-            nc.sync.dma_start(out=out.rearrange("(p c) d -> p c d", c=CHUNKS)[:, chunks[s], :], in_=rows[:])
+            copy(out=rows[:, chunks[s], :], in_=back[:])
 
-        for s in range(STAGES - 1):
-            store_rows(z_t, s, nc.scalar.copy, psum_acc, "acc", out_0)
+        def store(out, rows, first, last):
+            nc.sync.dma_start(
+                out=out.rearrange("(p c) d -> p c d", c=CHUNKS)[:, first:last, :], in_=rows[:, first:last, :]
+            )
+
+        z_rows = keep.tile([P, CHUNKS, D], F32)
+        zx_rows = keep.tile([P, CHUNKS, D], F32)
+        back_to_rows(z_t, 0, nc.vector.tensor_copy, psum_acc, "acc", z_rows)
+        back_to_rows(z_t, 1, nc.scalar.copy, psum_acc, "acc", z_rows)
+        store(out_0, z_rows, 0, CHUNKS // 2)
+        for s in (2, 3):
+            back_to_rows(z_t, s, nc.scalar.copy, psum_acc, "acc", z_rows)
+        store(out_0, z_rows, CHUNKS // 2, CHUNKS)
         for s in range(STAGES):
             nc.vector.tensor_scalar(
                 out=zx_t[:, cols[s]],
@@ -371,6 +392,6 @@ def tile_modelvd_pa_kernel(tc, en1, W2, b2, Wmean, Wlogvar, eps, out_0, out_1):
                 op0=ALU.add,
                 op1=ALU.mult,
             )
-        store_rows(z_t, STAGES - 1, nc.vector.tensor_copy, psum_acc, "acc", out_0)
         for s in range(STAGES):
-            store_rows(zx_t, s, (nc.scalar.copy, nc.vector.tensor_copy)[s % 2], psum_flip, "flip", out_1)
+            back_to_rows(zx_t, s, (nc.scalar.copy, nc.vector.tensor_copy)[s % 2], psum_flip, "flip", zx_rows)
+            store(out_1, zx_rows, s * CHUNKS_PER_STAGE, (s + 1) * CHUNKS_PER_STAGE)

@@ -218,9 +218,17 @@ def tile_modelvd_pa_kernel(tc, en1, W2, b2, Wmean, Wlogvar, eps, out_0, out_1):
                 out=raised, in0=raised, scalar1=BN_EPS * ROWS, scalar2=None, op0=ALU.add
             )
 
+        warm_head = psum_acc.tile([P, P], F32, tag="acc")
+
+        def warm(count):
+            for i in range(count):
+                nc.tensor.matmul(out=warm_head[:], lhsT=ident_bf16[:], rhs=ident_bf16[:], start=True, stop=True)
+
         regroup_w2(0)
         quantise_w2(0)
+        warm(14)
         flip_en1(0)
+        warm(8)
         regroup_w2(1)
         quantise_en1(0)
         quantise_w2(1)
@@ -363,6 +371,12 @@ def tile_modelvd_pa_kernel(tc, en1, W2, b2, Wmean, Wlogvar, eps, out_0, out_1):
             out=z_inv[:], in_=z_squares[:, 1:2], func=ACT.Abs_reciprocal_sqrt, bias=z_var_part[:], scale=1.0 / ROWS
         )
 
+        warm_tail = psum_acc.tile([P, P], F32, tag="acc")
+        for i in range(4):
+            nc.tensor.matmul(
+                out=warm_tail[:], lhsT=ident_f32[:], rhs=noise_t[:, STAGE : STAGE + P], start=True, stop=True
+            )
+
         def back_to_rows(values_t, s, copy, psum, tag, rows):
             back = psum.tile([P, CHUNKS_PER_STAGE, D], F32, tag=tag)
             for i in range(CHUNKS_PER_STAGE):
@@ -383,6 +397,8 @@ def tile_modelvd_pa_kernel(tc, en1, W2, b2, Wmean, Wlogvar, eps, out_0, out_1):
         for s in (2, 3):
             back_to_rows(z_t, s, nc.scalar.copy, psum_acc, "acc", z_rows)
         store(out_0, z_rows, CHUNKS // 2, CHUNKS)
+        for i in range(2):
+            nc.tensor.matmul(out=warm_tail[:], lhsT=ident_f32[:], rhs=noise_t[:, 0:P], start=True, stop=True)
         for s in range(STAGES):
             nc.vector.tensor_scalar(
                 out=zx_t[:, cols[s]],

from contextlib import ExitStack

import concourse.mybir as mybir
from concourse.masks import make_identity

F32 = mybir.dt.float32
BF16 = mybir.dt.bfloat16
U32 = mybir.dt.uint32
U8 = mybir.dt.uint8
FP8X4 = mybir.dt.float8_e4m3fn_x4
ALU = mybir.AluOpType
ACT = mybir.ActivationFunctionType

P = 128
PACK = 4
K_PASS = P * PACK

ROWS, EN1, EN2, D = 1024, 1024, 512, 128
BN_EPS = 1e-5

CHUNKS = ROWS // P
STAGE = 256
STAGES = ROWS // STAGE
CHUNKS_PER_STAGE = STAGE // P
PASSES1 = EN1 // K_PASS
E_TILES = EN2 // P
W2_SPLIT = 84
HALVES = 2
RUN = 4

MEAN, LOGVAR = 0, 1
BN_STATS_DIM = 6

FLOPS = 2 * ROWS * EN1 * EN2 + 2 * 2 * ROWS * EN2 * D


def regroup(copy, grouped, planes):
    copy(
        out=grouped.rearrange("p (c i) t -> p c t i", i=RUN),
        in_=planes.rearrange("p t (c i) -> p c t i", i=RUN),
    )


def tile_modelvd_pa_kernel(tc, en1, W2, b2, Wmean, Wlogvar, eps, out_0, out_1):
    nc = tc.nc
    with ExitStack() as ctx:
        ctx.enter_context(tc.manual_schedule())
        keep = ctx.enter_context(tc.tile_pool(name="keep", bufs=1))
        stage_pool = ctx.enter_context(tc.tile_pool(name="stage_pool", bufs=2))
        psum_flip = ctx.enter_context(tc.psum_pool(name="psum_flip", bufs=4))
        psum_acc = ctx.enter_context(tc.psum_pool(name="psum_acc", bufs=4))

        ident_f32 = keep.tile([P, P], F32)
        make_identity(nc, ident_f32[:])
        ident_bf16 = keep.tile([P, P], BF16)
        make_identity(nc, ident_bf16[:])
        minus_half = keep.tile([P, 1], F32)
        nc.vector.memset(minus_half[:], -0.5)
        epsilon = keep.tile([P, 1], F32)
        nc.vector.tensor_scalar(
            out=epsilon[:], in0=minus_half[:], scalar1=0.0, scalar2=BN_EPS, op0=ALU.mult, op1=ALU.add
        )
        table_warmer = keep.tile([P, 1], F32)
        nc.scalar.activation(out=table_warmer[:], in_=minus_half[:], func=ACT.Exp)

        w2_raw = keep.tile([P, PASSES1, PACK, EN2], BF16)

        def load_w2(g):
            nc.sync.dma_start(
                out=w2_raw[:, g],
                in_=W2[g * K_PASS : (g + 1) * K_PASS, :].rearrange("(q j) c -> q j c", j=PACK),
            )

        b2_raw = keep.tile([P, E_TILES], BF16)
        en1_sb = keep.tile([P, CHUNKS, EN1], BF16)
        en1_rows = en1.rearrange("(p c) k -> p c k", c=CHUNKS)
        head_raw = keep.tile([P, 2, PACK, D], BF16)
        eps_sb = keep.tile([P, CHUNKS, D], BF16)

        def load_en1(first, last):
            nc.sync.dma_start(out=en1_sb[:, first:last, :], in_=en1_rows[:, first:last, :])

        load_w2(0)
        load_en1(0, 1)
        load_en1(1, 2)
        load_w2(1)
        nc.sync.dma_start(out=b2_raw[:], in_=b2.rearrange("(p t) -> p t", t=E_TILES))
        load_en1(2, 4)
        nc.sync.dma_start(out=head_raw[:, MEAN], in_=Wmean.rearrange("(p t) d -> p t d", t=PACK))
        nc.sync.dma_start(out=head_raw[:, LOGVAR], in_=Wlogvar.rearrange("(p t) d -> p t d", t=PACK))
        load_en1(4, 6)
        load_en1(6, 8)
        nc.sync.dma_start(out=eps_sb[:], in_=eps.rearrange("(p c) d -> p c d", c=CHUNKS))

        w2_grouped = keep.tile([P, PASSES1, EN2, PACK], BF16, align_bytes=64)
        w2_codes = keep.tile([P, PASSES1, EN2], U32, align_bytes=64)
        w2_scales = keep.tile([P, PASSES1, EN2], U8, align_bytes=64)

        def regroup_w2(g):
            grouped = w2_grouped[:, g].rearrange("q (t m) j -> q m j t", t=E_TILES)
            raw = w2_raw[:, g].rearrange("q j (m t) -> q m j t", t=E_TILES)
            nc.vector.tensor_copy(out=grouped[:, 0:W2_SPLIT], in_=raw[:, 0:W2_SPLIT])
            nc.scalar.copy(out=grouped[:, W2_SPLIT:P], in_=raw[:, W2_SPLIT:P])

        def quantise_w2(g):
            nc.vector.quantize_mx(
                out=w2_codes[:, g, :].bitcast(FP8X4),
                scales=w2_scales[:, g, :],
                in_=w2_grouped[:, g].rearrange("q c t -> q (c t)"),
            )

        head_codes = keep.tile([P, 2, D], U32, align_bytes=64)
        head_scales = keep.tile([P, 2, D], U8, align_bytes=64)

        def quantise_head_weights():
            head_grouped = keep.tile([P, 2, D, PACK], BF16, align_bytes=64)
            for w in (MEAN, LOGVAR):
                regroup(nc.vector.tensor_copy, head_grouped[:, w], head_raw[:, w])
            nc.vector.quantize_mx(
                out=head_codes[:].rearrange("p w d -> p (w d)").bitcast(FP8X4),
                scales=head_scales[:].rearrange("p w d -> p (w d)"),
                in_=head_grouped[:].rearrange("p w d t -> p (w d t)"),
            )

        en1_codes = keep.tile([P, STAGES, PASSES1, STAGE], U32, align_bytes=64)
        en1_scales = keep.tile([P, STAGES, PASSES1, STAGE], U8, align_bytes=64)
        en2_codes = keep.tile([P, ROWS], U32, align_bytes=64)
        en2_scales = keep.tile([P, ROWS], U8, align_bytes=64)
        b2_col = keep.tile([P, E_TILES], F32)
        stats = keep.tile([P, 2, STAGES, BN_STATS_DIM], F32)
        en1_grouped, acc, en2_planes, en2_grouped, head_out = {}, {}, {}, {}, {}

        def flip_en1(s):
            en1_grouped[s] = stage_pool.tile(
                [P, PASSES1, STAGE, PACK], BF16, name="en1_grouped%d" % s, tag="en1_grouped", align_bytes=64
            )
            for i in range(CHUNKS_PER_STAGE):
                words = en1_sb[:, s * CHUNKS_PER_STAGE + i, :].bitcast(F32)
                flipped = psum_flip.tile([P, PASSES1, HALVES, P], F32, tag="flip")
                for g in range(PASSES1):
                    for u in range(HALVES):
                        words_u = words[:, g * HALVES * P + u : (g + 1) * HALVES * P : HALVES]
                        nc.tensor.transpose(flipped[:, g, u, :], words_u, ident_f32[:])
                nc.scalar.copy(
                    out=en1_grouped[s][:, :, i * P : (i + 1) * P, :].bitcast(F32),
                    in_=flipped[:].rearrange("q g u n -> q g n u"),
                )

        def quantise_en1(s):
            nc.vector.quantize_mx(
                out=en1_codes[:, s].rearrange("q g n -> q (g n)").bitcast(FP8X4),
                scales=en1_scales[:, s].rearrange("q g n -> q (g n)"),
                in_=en1_grouped[s][:].rearrange("q g n t -> q (g n t)"),
            )

        def multiply(s, rows=(0, STAGE)):
            first, last = rows
            for t in range(E_TILES):
                e_cols = slice(t * P, (t + 1) * P)
                acc[s, t] = psum_acc.tile([P, last - first], F32, name="acc%d%d" % (s, t), tag="acc")
                for g in range(PASSES1):
                    nc.tensor.matmul_mx(
                        out=acc[s, t][:],
                        lhsT=w2_codes[:, g, e_cols].bitcast(FP8X4),
                        lhsT_scale=w2_scales[:, g, e_cols],
                        rhs=en1_codes[:, s, g, first:last].bitcast(FP8X4),
                        rhs_scale=en1_scales[:, s, g, first:last],
                        start=(g == 0),
                        stop=(g == PASSES1 - 1),
                    )

        def bias_and_relu(s, rows=(0, STAGE)):
            first, last = rows
            if first == 0:
                en2_planes[s] = stage_pool.tile([P, E_TILES, STAGE], BF16, name="en2_planes%d" % s, tag="en2_planes")
            for t in range(E_TILES):
                nc.scalar.activation(
                    out=en2_planes[s][:, t, first:last], in_=acc[s, t][:], func=ACT.Relu, bias=b2_col[:, t : t + 1], scale=1.0
                )

        def regroup_en2(s, rows=(0, STAGE)):
            first, last = rows
            if first == 0:
                en2_grouped[s] = stage_pool.tile([P, STAGE, PACK], BF16, name="en2_grouped%d" % s, tag="en2_grouped", align_bytes=64)
            regroup(nc.vector.tensor_copy, en2_grouped[s][:, first:last, :], en2_planes[s][:, :, first:last])

        def quantise_en2(s, rows=(0, STAGE)):
            first, last = rows
            stage_cols = slice(s * STAGE + first, s * STAGE + last)
            nc.vector.quantize_mx(
                out=en2_codes[:, stage_cols].bitcast(FP8X4),
                scales=en2_scales[:, stage_cols],
                in_=en2_grouped[s][:, first:last, :].rearrange("p n t -> p (n t)"),
            )

        def heads(s, rows=(0, STAGE)):
            first, last = rows
            stage_cols = slice(s * STAGE + first, s * STAGE + last)
            if first == 0:
                head_out[s] = psum_flip.tile([P, 2, STAGE], F32, name="head_out%d" % s, tag="flip")
            for w in (LOGVAR, MEAN):
                nc.tensor.matmul_mx(
                    out=head_out[s][:, w, first:last],
                    lhsT=head_codes[:, w, :].bitcast(FP8X4),
                    lhsT_scale=head_scales[:, w, :],
                    rhs=en2_codes[:, stage_cols].bitcast(FP8X4),
                    rhs_scale=en2_scales[:, stage_cols],
                    start=True,
                    stop=True,
                )

        def head_stats(s, w):
            nc.vector.bn_stats(out=stats[:, w, s, :], in_=head_out[s][:, w, :])

        def add_epsilon():
            raised = stats[:, MEAN : LOGVAR + 1, 0, 2]
            nc.vector.tensor_scalar(
                out=raised, in0=raised, scalar1=BN_EPS * ROWS, scalar2=None, op0=ALU.add
            )

        warm_head = psum_acc.tile([P, P], F32, tag="acc")

        def warm(count):
            for i in range(count):
                nc.tensor.matmul(out=warm_head[:], lhsT=ident_bf16[:], rhs=ident_bf16[:], start=True, stop=True)

        regroup_w2(0)
        quantise_w2(0)
        warm(14)
        flip_en1(0)
        warm(8)
        regroup_w2(1)
        quantise_en1(0)
        quantise_w2(1)
        nc.vector.tensor_copy(out=b2_col[:], in_=b2_raw[:])
        flip_en1(1)
        multiply(0)
        quantise_head_weights()
        quantise_en1(1)
        bias_and_relu(0)
        flip_en1(2)
        regroup_en2(0)
        quantise_en1(2)
        quantise_en2(0)
        flip_en1(3)
        multiply(1)
        bias_and_relu(1)
        heads(0)
        multiply(2)
        quantise_en1(3)
        head_stats(0, LOGVAR)
        head_stats(0, MEAN)
        regroup_en2(1)
        add_epsilon()
        bias_and_relu(2)
        multiply(3, (0, P))
        bias_and_relu(3, (0, P))
        multiply(3, (P, STAGE))
        bias_and_relu(3, (P, STAGE))
        quantise_en2(1)
        heads(1)
        eps_flipped = psum_acc.tile([P, CHUNKS, P], BF16, tag="acc")
        for c in range(CHUNKS):
            nc.tensor.transpose(eps_flipped[:, c, :], eps_sb[:, c, :], ident_bf16[:])
        regroup_en2(2)
        quantise_en2(2)
        heads(2)
        regroup_en2(3, (0, P))
        regroup_en2(3, (P, STAGE))
        quantise_en2(3, (0, P))
        quantise_en2(3, (P, STAGE))
        heads(3, (0, P))
        heads(3, (P, STAGE))
        head_stats(1, LOGVAR)
        head_stats(2, LOGVAR)
        head_stats(3, LOGVAR)

        lv_mean_var = keep.tile([P, 2], F32)
        lv_inv = keep.tile([P, 1], F32)
        lv_half_inv = keep.tile([P, 1], F32)
        lv_minus_half_mean = keep.tile([P, 1], F32)
        lv_bias = keep.tile([P, 1], F32)
        m_mean_var = keep.tile([P, 2], F32)
        m_inv = keep.tile([P, 1], F32)
        m_minus_mean = keep.tile([P, 1], F32)
        m_bias = keep.tile([P, 1], F32)
        noise_sums = keep.tile([P, STAGES], F32)
        noise_sum = keep.tile([P, 1], F32)
        centre = keep.tile([P, 1], F32)
        z_squares = keep.tile([P, 2], F32)
        z_var_part = keep.tile([P, 1], F32)
        z_inv = keep.tile([P, 1], F32)

        def aggregate(mean_var, w):
            nc.vector.bn_aggr(out=mean_var[:], in_=stats[:, w].rearrange("p s f -> p (s f)"))

        def inverse_sqrt(inv, mean_var):
            nc.gpsimd.tensor_tensor(out=inv[:], in0=mean_var[:, 1:2], in1=minus_half[:], op=ALU.pow)

        aggregate(lv_mean_var, LOGVAR)
        inverse_sqrt(lv_inv, lv_mean_var)
        head_stats(1, MEAN)
        head_stats(2, MEAN)
        nc.vector.tensor_scalar_mul(out=lv_minus_half_mean[:], in0=lv_mean_var[:, 0:1], scalar1=-0.5)
        head_stats(3, MEAN)
        nc.scalar.activation(out=lv_half_inv[:], in_=lv_inv[:], func=ACT.Copy, scale=0.5)
        nc.scalar.activation(out=lv_bias[:], in_=lv_minus_half_mean[:], func=ACT.Copy, scale=lv_inv[:])
        aggregate(m_mean_var, MEAN)
        inverse_sqrt(m_inv, m_mean_var)
        nc.vector.tensor_scalar_mul(out=m_minus_mean[:], in0=m_mean_var[:, 0:1], scalar1=-1.0)
        nc.gpsimd.tensor_tensor(out=m_bias[:], in0=m_minus_mean[:], in1=m_inv[:], op=ALU.mult)

        noise_t = keep.tile([P, ROWS], F32)
        y_t = keep.tile([P, ROWS], F32)
        z_t = keep.tile([P, ROWS], F32)
        zx_t = keep.tile([P, ROWS], F32)
        squares = keep.tile([P, ROWS], F32)
        cols = [slice(s * STAGE, (s + 1) * STAGE) for s in range(STAGES)]
        chunks = [slice(s * CHUNKS_PER_STAGE, (s + 1) * CHUNKS_PER_STAGE) for s in range(STAGES)]

        for s in range(STAGES):
            nc.scalar.activation(
                out=noise_t[:, cols[s]],
                in_=head_out[s][:, LOGVAR, :],
                func=ACT.Exp,
                bias=lv_bias[:],
                scale=lv_half_inv[:],
            )
        nc.scalar.activation(out=table_warmer[:], in_=epsilon[:], func=ACT.Abs_reciprocal_sqrt)
        for s in range(STAGES):
            nc.vector.scalar_tensor_tensor(
                out=noise_t[:, cols[s]],
                in0=noise_t[:, cols[s]],
                scalar=1.0,
                in1=eps_flipped[:, chunks[s], :].rearrange("d c n -> d (c n)"),
                op0=ALU.mult,
                op1=ALU.mult,
                accum_out=noise_sums[:, s : s + 1],
            )
        for s in range(STAGES):
            nc.vector.scalar_tensor_tensor(
                out=y_t[:, cols[s]],
                in0=head_out[s][:, MEAN, :],
                scalar=m_inv[:],
                in1=noise_t[:, cols[s]],
                op0=ALU.mult,
                op1=ALU.add,
            )
            if s == 0:
                nc.vector.tensor_reduce(out=noise_sum[:], in_=noise_sums[:], op=ALU.add, axis=mybir.AxisListType.X)
            if s == 1:
                nc.vector.scalar_tensor_tensor(
                    out=centre[:], in0=noise_sum[:], scalar=-1.0 / ROWS, in1=m_bias[:], op0=ALU.mult, op1=ALU.add
                )
        for h in range(2):
            half = slice(h * ROWS // 2, (h + 1) * ROWS // 2)
            nc.scalar.activation(
                out=squares[:, half],
                in_=y_t[:, half],
                func=ACT.Square,
                bias=centre[:],
                scale=1.0,
                accum_out=z_squares[:, h : h + 1],
            )
        for s in range(STAGES):
            nc.vector.tensor_scalar(out=z_t[:, cols[s]], in0=y_t[:, cols[s]], scalar1=m_bias[:], scalar2=None, op0=ALU.add)
        nc.vector.tensor_scalar(
            out=z_var_part[:], in0=z_squares[:, 0:1], scalar1=1.0 / ROWS, scalar2=BN_EPS, op0=ALU.mult, op1=ALU.add
        )
        nc.scalar.activation(
            out=z_inv[:], in_=z_squares[:, 1:2], func=ACT.Abs_reciprocal_sqrt, bias=z_var_part[:], scale=1.0 / ROWS
        )

        warm_tail = psum_acc.tile([P, P], F32, tag="acc")
        for i in range(4):
            nc.tensor.matmul(
                out=warm_tail[:], lhsT=ident_f32[:], rhs=noise_t[:, STAGE : STAGE + P], start=True, stop=True
            )

        def back_to_rows(values_t, s, copy, psum, tag, rows):
            back = psum.tile([P, CHUNKS_PER_STAGE, D], F32, tag=tag)
            for i in range(CHUNKS_PER_STAGE):
                first = s * STAGE + i * P
                nc.tensor.transpose(back[:, i, :], values_t[:, first : first + P], ident_f32[:])
            copy(out=rows[:, chunks[s], :], in_=back[:])

        def store(out, rows, first, last):
            nc.sync.dma_start(
                out=out.rearrange("(p c) d -> p c d", c=CHUNKS)[:, first:last, :], in_=rows[:, first:last, :]
            )

        z_rows = keep.tile([P, CHUNKS, D], F32)
        zx_rows = keep.tile([P, CHUNKS, D], F32)
        back_to_rows(z_t, 0, nc.vector.tensor_copy, psum_acc, "acc", z_rows)
        back_to_rows(z_t, 1, nc.scalar.copy, psum_acc, "acc", z_rows)
        store(out_0, z_rows, 0, CHUNKS // 2)
        for s in (2, 3):
            back_to_rows(z_t, s, nc.scalar.copy, psum_acc, "acc", z_rows)
        store(out_0, z_rows, CHUNKS // 2, CHUNKS)
        for i in range(2):
            nc.tensor.matmul(out=warm_tail[:], lhsT=ident_f32[:], rhs=noise_t[:, 0:P], start=True, stop=True)
        for s in range(STAGES):
            nc.vector.tensor_scalar(
                out=zx_t[:, cols[s]],
                in0=y_t[:, cols[s]],
                scalar1=centre[:],
                scalar2=z_inv[:],
                op0=ALU.add,
                op1=ALU.mult,
            )
        for s in range(STAGES):
            back_to_rows(zx_t, s, (nc.scalar.copy, nc.vector.tensor_copy)[s % 2], psum_flip, "flip", zx_rows)
            store(out_1, zx_rows, s * CHUNKS_PER_STAGE, (s + 1) * CHUNKS_PER_STAGE)
